import numpy as np
import ml_dtypes


def mxq(x, axis, fmt="e4m3"):
    dtype, down = {"e4m3": (ml_dtypes.float8_e4m3fn, 7), "e5m2": (ml_dtypes.float8_e5m2, 14)}[fmt]
    v = np.moveaxis(np.asarray(x, np.float32).astype(ml_dtypes.bfloat16).astype(np.float64), axis, -1)
    blocks = v.reshape(v.shape[:-1] + (-1, 32))
    amax = np.abs(blocks).max(-1, keepdims=True)
    byte = np.maximum(np.where(amax > 0, np.frexp(amax)[1] - 1 + 127, 0) - down, 1)
    scale = np.exp2(byte - 127.0)
    codes = (blocks / scale).astype(np.float32).astype(dtype).astype(np.float64)
    return np.moveaxis((codes * scale).reshape(v.shape), -1, axis)


WIDE = False


def mx_kscale(k):
    if not WIDE:
        return np.ones(k)
    levels = np.array([10, -10, 5, -5, 0])
    a = np.random.permutation(np.resize(levels, k // 512 * 4)).reshape(k // 512, 4)
    idx = np.arange(k)
    return np.exp2(a[idx // 512, idx % 128 // 32])


BF16 = ml_dtypes.bfloat16


def bf(x):
    return np.asarray(x, np.float32).astype(BF16)


def f64(x):
    return np.asarray(x).astype(np.float64)


B, C, TC, H, W = 4, 512, 512, 32, 16
N = H * W
EPS = 1e-6


def setup_inputs():
    s = mx_kscale(TC)
    return {"token": bf(np.random.standard_normal((B, TC, H, W)) * s[None, :, None, None]),
            "Wk": bf(np.random.standard_normal((C, TC)) / np.sqrt(TC) / s[None, :]),
            "Wv": bf(np.random.standard_normal((C, TC)) * 3.0 / np.sqrt(TC) / s[None, :])}


def reference(token, Wk, Wv):
    tq = mxq(f64(token).reshape(B, TC, N), 1, "e4m3")
    kf = mxq(f64(Wk), 1, "e4m3") @ tq
    v = mxq(f64(Wv), 1, "e4m3") @ tq
    vf = v.transpose(0, 2, 1)
    kn = kf / np.maximum(np.sqrt((kf * kf).sum(1, keepdims=True)), EPS)
    return kn, vf

@@ -1,0 +1,163 @@
+import concourse.mybir as mybir
+from concourse.masks import make_identity
+
+BF16 = mybir.dt.bfloat16
+F32 = mybir.dt.float32
+U32 = mybir.dt.uint32
+U8 = mybir.dt.uint8
+FP8X4 = mybir.dt.float8_e4m3fn_x4
+ACT = mybir.ActivationFunctionType
+
+P = 128
+PACK = 4
+IMAGES = 4
+IN_CH = P * PACK
+OUT_CH = 512
+PIXELS = 512
+CHUNKS = 4
+EPS = 1e-6
+
+FLOPS = 2 * 2 * IMAGES * OUT_CH * IN_CH * PIXELS
+
+
+def tile_trgramkqv_pa_kernel(tc, token, Wk, Wv, out_0, out_1):
+    nc = tc.nc
+    kn_out, vf_out = out_0, out_1
+
+    with tc.tile_pool(name="consts", bufs=1) as consts, tc.tile_pool(
+        name="weights", bufs=2
+    ) as weights, tc.tile_pool(name="images", bufs=IMAGES) as images, tc.psum_pool(
+        name="to_scalar", bufs=4
+    ) as to_scalar, tc.psum_pool(name="to_vector", bufs=4) as to_vector, tc.manual_schedule():
+        wk_raw = weights.tile([P, CHUNKS * IN_CH], BF16, name="w_raw", tag="w_raw")
+        nc.sync.dma_start(out=wk_raw[:], in_=Wk.rearrange("(p j) k -> p (j k)", j=CHUNKS))
+        tok_raw = [images.tile([P, PACK * PIXELS], BF16, name="tok_raw", tag="tok_raw") for b in range(IMAGES)]
+        nc.sync.dma_start(out=tok_raw[0][:], in_=token[0].rearrange("(p t) h w -> p (t h w)", t=PACK))
+        wv_raw = weights.tile([P, CHUNKS * IN_CH], BF16, name="w_raw", tag="w_raw")
+        nc.sync.dma_start(
+            out=wv_raw[:].rearrange("p (j k) -> p j k", j=CHUNKS),
+            in_=Wv.rearrange("(j p) k -> p j k", p=P),
+        )
+        for b in range(1, IMAGES):
+            nc.sync.dma_start(out=tok_raw[b][:], in_=token[b].rearrange("(p t) h w -> p (t h w)", t=PACK))
+
+        ident = consts.tile([P, P], F32)
+        make_identity(nc, ident[:])
+
+        minus_half = consts.tile([P, CHUNKS], F32)
+        nc.gpsimd.memset(minus_half[:], -0.5)
+
+        def transpose_weight(raw):
+            words = raw[:].bitcast(F32).rearrange("c (j p u) -> c j u p", j=CHUNKS, u=2)
+            grouped = weights.tile([P, OUT_CH * PACK], BF16, align_bytes=64, name="w_grouped", tag="w_grouped")
+            grouped_words = grouped[:].bitcast(F32).rearrange("p (c u) -> p c u", u=2)
+            for half in range(2):
+                bank = to_scalar.tile([P, 2, 2 * P], F32, name="w_bank", tag="bank")
+                for jj in range(2):
+                    for u in range(2):
+                        nc.tensor.transpose(
+                            bank[:, u, P * jj : P * (jj + 1)], words[:, 2 * half + jj, u, :], ident[:]
+                        )
+                nc.scalar.copy(
+                    out=grouped_words[:, 2 * P * half : 2 * P * (half + 1), :],
+                    in_=bank[:].rearrange("p u c -> p c u"),
+                )
+            return grouped
+
+        def regroup_token(b):
+            grouped = images.tile([P, PIXELS * PACK], BF16, align_bytes=64, name="tok_grouped", tag="tok_grouped")
+            nc.vector.tensor_copy(
+                out=grouped[:].rearrange("p (c i t) -> p c t i", i=4, t=PACK),
+                in_=tok_raw[b][:].rearrange("p (t c i) -> p c t i", t=PACK, i=4),
+            )
+            return grouped
+
+        def quantise(grouped, pool):
+            codes = pool.tile([P, 512], U32, align_bytes=64, name="codes", tag="codes")
+            scales = pool.tile([P, 512], U8, align_bytes=64, name="scales", tag="scales")
+            nc.vector.quantize_mx(out=codes[:].bitcast(FP8X4), scales=scales[:], in_=grouped[:])
+            return codes, scales
+
+        def product(acc, stationary, columns, moving):
+            nc.tensor.matmul_mx(
+                out=acc[:],
+                lhsT=stationary[0][:, columns].bitcast(FP8X4),
+                lhsT_scale=stationary[1][:, columns],
+                rhs=moving[0][:].bitcast(FP8X4),
+                rhs_scale=moving[1][:],
+                start=True,
+                stop=True,
+            )
+
+        tok = {}
+        v_sb = [images.tile([P, CHUNKS, OUT_CH], F32, name="v_sb", tag="v_sb") for b in range(IMAGES)]
+        kn_sb = [images.tile([P, CHUNKS, PIXELS], F32, name="kn_sb", tag="kn_sb") for b in range(IMAGES)]
+        squares = [images.tile([P, CHUNKS, OUT_CH], F32, name="squares", tag="squares") for b in range(IMAGES)]
+        sumsq = [images.tile([P, CHUNKS], F32, name="sumsq", tag="sumsq") for b in range(IMAGES)]
+        inv_row = [images.tile([P, PIXELS], F32, name="inv_row", tag="inv_row") for b in range(IMAGES)]
+
+        def value_chunk(b, i):
+            pixels = slice(P * i, P * (i + 1))
+            if i == CHUNKS - 1:
+                acc = to_vector.tile([P, OUT_CH], F32, name="v_acc", tag="bank")
+                product(acc, tok[b], pixels, wv)
+                nc.vector.tensor_copy(out=v_sb[b][:, i, :], in_=acc[:])
+            else:
+                acc = to_scalar.tile([P, OUT_CH], F32, name="v_acc", tag="bank")
+                product(acc, tok[b], pixels, wv)
+                nc.scalar.copy(out=v_sb[b][:, i, :], in_=acc[:])
+            nc.sync.dma_start(out=vf_out[b, pixels, :], in_=v_sb[b][:, i, :])
+
+        def sumsq_chunk(b, i):
+            acc = to_scalar.tile([P, OUT_CH], F32, name="kt_acc", tag="bank")
+            product(acc, tok[b], slice(P * i, P * (i + 1)), wk)
+            nc.scalar.activation(
+                out=squares[b][:, i, :], in_=acc[:], func=ACT.Square, accum_out=sumsq[b][:, i : i + 1]
+            )
+
+        def spread_inverse_norm(b):
+            clamped = images.tile([P, CHUNKS], F32, name="clamped", tag="clamped")
+            nc.gpsimd.tensor_scalar_max(out=clamped[:], in0=sumsq[b][:], scalar1=EPS * EPS)
+            inverse = images.tile([P, CHUNKS], F32, name="inverse", tag="inverse")
+            nc.gpsimd.tensor_tensor(out=inverse[:], in0=clamped[:], in1=minus_half[:], op=mybir.AluOpType.pow)
+            spread = to_vector.tile([P, PIXELS], F32, name="spread", tag="bank")
+            for i in range(CHUNKS):
+                nc.tensor.transpose(
+                    spread[:, P * i : P * (i + 1)], inverse[:, i : i + 1].to_broadcast([P, P]), ident[:]
+                )
+            nc.vector.tensor_copy(out=inv_row[b][:], in_=spread[:])
+
+        def key_chunk(b, j):
+            acc = to_vector.tile([P, PIXELS], F32, name="k_acc", tag="bank")
+            product(acc, wk, slice(P * j, P * (j + 1)), tok[b])
+            nc.vector.tensor_mul(out=kn_sb[b][:, j, :], in0=acc[:], in1=inv_row[b][:])
+            if j % 2 == 1:
+                kn_rows = kn_out[b].rearrange("(p j) n -> p j n", j=CHUNKS)
+                nc.sync.dma_start(out=kn_rows[:, j - 1 : j + 1, :], in_=kn_sb[b][:, j - 1 : j + 1, :])
+
+        wk_grouped = transpose_weight(wk_raw)
+        tok_grouped = [regroup_token(0)]
+        wk = quantise(wk_grouped, weights)
+        tok[0] = quantise(tok_grouped[0], images)
+        wv_grouped = transpose_weight(wv_raw)
+        tok_grouped.append(regroup_token(1))
+        wv = quantise(wv_grouped, weights)
+        for i in range(CHUNKS):
+            sumsq_chunk(0, i)
+        tok[1] = quantise(tok_grouped[1], images)
+        tok_grouped.append(regroup_token(2))
+        for b in range(IMAGES):
+            for i in range(CHUNKS):
+                value_chunk(b, i)
+            if b + 2 < IMAGES:
+                tok[b + 2] = quantise(tok_grouped[b + 2], images)
+            if b + 3 < IMAGES:
+                tok_grouped.append(regroup_token(b + 3))
+            if b + 1 < IMAGES:
+                sumsq_chunk(b + 1, 0)
+            spread_inverse_norm(b)
+            key_chunk(b, 0)
+            for i in range(1, CHUNKS):
+                if b + 1 < IMAGES:
+                    sumsq_chunk(b + 1, i)
+                key_chunk(b, i)

@@ -44,8 +44,10 @@ def tile_trgramkqv_pa_kernel(tc, token, Wk, Wv, out_0, out_1):
         ident = consts.tile([P, P], F32)
         make_identity(nc, ident[:])
 
-        minus_half = consts.tile([P, CHUNKS], F32)
-        nc.gpsimd.memset(minus_half[:], -0.5)
+        one = consts.tile([P, 1], F32)
+        nc.vector.memset(one[:], 1.0)
+        warm = consts.tile([P, 1], F32)
+        nc.scalar.activation(out=warm[:], in_=one[:], func=ACT.Abs_reciprocal_sqrt)
 
         def transpose_weight(raw):
             words = raw[:].bitcast(F32).rearrange("c (j p u) -> c j u p", j=CHUNKS, u=2)
@@ -98,7 +100,7 @@ def tile_trgramkqv_pa_kernel(tc, token, Wk, Wv, out_0, out_1):
 
         def value_chunk(b, i):
             pixels = slice(P * i, P * (i + 1))
-            if i == CHUNKS - 1:
+            if i >= CHUNKS // 2:
                 acc = to_vector.tile([P, OUT_CH], F32, name="v_acc", tag="bank")
                 product(acc, tok[b], pixels, wv)
                 nc.vector.tensor_copy(out=v_sb[b][:, i, :], in_=acc[:])
@@ -116,29 +118,32 @@ def tile_trgramkqv_pa_kernel(tc, token, Wk, Wv, out_0, out_1):
             )
 
         def spread_inverse_norm(b):
-            clamped = images.tile([P, CHUNKS], F32, name="clamped", tag="clamped")
-            nc.gpsimd.tensor_scalar_max(out=clamped[:], in0=sumsq[b][:], scalar1=EPS * EPS)
-            inverse = images.tile([P, CHUNKS], F32, name="inverse", tag="inverse")
-            nc.gpsimd.tensor_tensor(out=inverse[:], in0=clamped[:], in1=minus_half[:], op=mybir.AluOpType.pow)
-            spread = to_vector.tile([P, PIXELS], F32, name="spread", tag="bank")
+            spread = to_scalar.tile([P, PIXELS], F32, name="spread", tag="bank")
             for i in range(CHUNKS):
                 nc.tensor.transpose(
-                    spread[:, P * i : P * (i + 1)], inverse[:, i : i + 1].to_broadcast([P, P]), ident[:]
+                    spread[:, P * i : P * (i + 1)], sumsq[b][:, i : i + 1].to_broadcast([P, P]), ident[:]
                 )
-            nc.vector.tensor_copy(out=inv_row[b][:], in_=spread[:])
+            nc.scalar.activation(out=inv_row[b][:], in_=spread[:], func=ACT.Abs_reciprocal_sqrt)
 
         def key_chunk(b, j):
             acc = to_vector.tile([P, PIXELS], F32, name="k_acc", tag="bank")
             product(acc, wk, slice(P * j, P * (j + 1)), tok[b])
-            nc.vector.tensor_mul(out=kn_sb[b][:, j, :], in0=acc[:], in1=inv_row[b][:])
+            nc.vector.scalar_tensor_tensor(
+                out=kn_sb[b][:, j, :],
+                in0=inv_row[b][:],
+                scalar=1.0 / EPS,
+                in1=acc[:],
+                op0=mybir.AluOpType.min,
+                op1=mybir.AluOpType.mult,
+            )
             if j % 2 == 1:
                 kn_rows = kn_out[b].rearrange("(p j) n -> p j n", j=CHUNKS)
                 nc.sync.dma_start(out=kn_rows[:, j - 1 : j + 1, :], in_=kn_sb[b][:, j - 1 : j + 1, :])
 
         wk_grouped = transpose_weight(wk_raw)
         tok_grouped = [regroup_token(0)]
-        wk = quantise(wk_grouped, weights)
         tok[0] = quantise(tok_grouped[0], images)
+        wk = quantise(wk_grouped, weights)
         wv_grouped = transpose_weight(wv_raw)
         tok_grouped.append(regroup_token(1))
         wv = quantise(wv_grouped, weights)
@@ -153,11 +158,8 @@ def tile_trgramkqv_pa_kernel(tc, token, Wk, Wv, out_0, out_1):
                 tok[b + 2] = quantise(tok_grouped[b + 2], images)
             if b + 3 < IMAGES:
                 tok_grouped.append(regroup_token(b + 3))
-            if b + 1 < IMAGES:
-                sumsq_chunk(b + 1, 0)
             spread_inverse_norm(b)
-            key_chunk(b, 0)
-            for i in range(1, CHUNKS):
+            for i in range(CHUNKS):
+                key_chunk(b, i)
                 if b + 1 < IMAGES:
                     sumsq_chunk(b + 1, i)
-                key_chunk(b, i)

@@ -68,10 +68,20 @@ def tile_trgramkqv_pa_kernel(tc, token, Wk, Wv, out_0, out_1):
 
         def regroup_token(b):
             grouped = images.tile([P, PIXELS * PACK], BF16, align_bytes=64, name="tok_grouped", tag="tok_grouped")
-            nc.vector.tensor_copy(
-                out=grouped[:].rearrange("p (c i t) -> p c t i", i=4, t=PACK),
-                in_=tok_raw[b][:].rearrange("p (t c i) -> p c t i", t=PACK, i=4),
-            )
+            if b < 2:
+                nc.vector.tensor_copy(
+                    out=grouped[:].rearrange("p (c i t) -> p c t i", i=4, t=PACK),
+                    in_=tok_raw[b][:].rearrange("p (t c i) -> p c t i", t=PACK, i=4),
+                )
+            else:
+                nc.gpsimd.tensor_scalar(
+                    out=grouped[:].rearrange("p (n t) -> p n t", t=PACK),
+                    in0=tok_raw[b][:].rearrange("p (t n) -> p n t", t=PACK),
+                    scalar1=1.0,
+                    scalar2=0.0,
+                    op0=mybir.AluOpType.mult,
+                    op1=mybir.AluOpType.add,
+                )
             return grouped
 
         def quantise(grouped, pool):

@@ -29,15 +29,15 @@ def tile_trgramkqv_pa_kernel(tc, token, Wk, Wv, out_0, out_1):
     ) as weights, tc.tile_pool(name="images", bufs=IMAGES) as images, tc.psum_pool(
         name="to_scalar", bufs=4
     ) as to_scalar, tc.psum_pool(name="to_vector", bufs=4) as to_vector, tc.manual_schedule():
-        wk_raw = weights.tile([P, CHUNKS * IN_CH], BF16, name="w_raw", tag="w_raw")
-        nc.sync.dma_start(out=wk_raw[:], in_=Wk.rearrange("(p j) k -> p (j k)", j=CHUNKS))
-        tok_raw = [images.tile([P, PACK * PIXELS], BF16, name="tok_raw", tag="tok_raw") for b in range(IMAGES)]
-        nc.sync.dma_start(out=tok_raw[0][:], in_=token[0].rearrange("(p t) h w -> p (t h w)", t=PACK))
         wv_raw = weights.tile([P, CHUNKS * IN_CH], BF16, name="w_raw", tag="w_raw")
         nc.sync.dma_start(
             out=wv_raw[:].rearrange("p (j k) -> p j k", j=CHUNKS),
             in_=Wv.rearrange("(j p) k -> p j k", p=P),
         )
+        tok_raw = [images.tile([P, PACK * PIXELS], BF16, name="tok_raw", tag="tok_raw") for b in range(IMAGES)]
+        nc.sync.dma_start(out=tok_raw[0][:], in_=token[0].rearrange("(p t) h w -> p (t h w)", t=PACK))
+        wk_raw = weights.tile([P, CHUNKS * IN_CH], BF16, name="w_raw", tag="w_raw")
+        nc.sync.dma_start(out=wk_raw[:], in_=Wk.rearrange("(p j) k -> p (j k)", j=CHUNKS))
         for b in range(1, IMAGES):
             nc.sync.dma_start(out=tok_raw[b][:], in_=token[b].rearrange("(p t) h w -> p (t h w)", t=PACK))
 
@@ -68,20 +68,10 @@ def tile_trgramkqv_pa_kernel(tc, token, Wk, Wv, out_0, out_1):
 
         def regroup_token(b):
             grouped = images.tile([P, PIXELS * PACK], BF16, align_bytes=64, name="tok_grouped", tag="tok_grouped")
-            if b < 2:
-                nc.vector.tensor_copy(
-                    out=grouped[:].rearrange("p (c i t) -> p c t i", i=4, t=PACK),
-                    in_=tok_raw[b][:].rearrange("p (t c i) -> p c t i", t=PACK, i=4),
-                )
-            else:
-                nc.gpsimd.tensor_scalar(
-                    out=grouped[:].rearrange("p (n t) -> p n t", t=PACK),
-                    in0=tok_raw[b][:].rearrange("p (t n) -> p n t", t=PACK),
-                    scalar1=1.0,
-                    scalar2=0.0,
-                    op0=mybir.AluOpType.mult,
-                    op1=mybir.AluOpType.add,
-                )
+            nc.vector.tensor_copy(
+                out=grouped[:].rearrange("p (c i t) -> p c t i", i=4, t=PACK),
+                in_=tok_raw[b][:].rearrange("p (t c i) -> p c t i", t=PACK, i=4),
+            )
             return grouped
 
         def quantise(grouped, pool):
@@ -150,24 +140,27 @@ def tile_trgramkqv_pa_kernel(tc, token, Wk, Wv, out_0, out_1):
                 kn_rows = kn_out[b].rearrange("(p j) n -> p j n", j=CHUNKS)
                 nc.sync.dma_start(out=kn_rows[:, j - 1 : j + 1, :], in_=kn_sb[b][:, j - 1 : j + 1, :])
 
-        wk_grouped = transpose_weight(wk_raw)
+        wv_grouped = transpose_weight(wv_raw)
         tok_grouped = [regroup_token(0)]
         tok[0] = quantise(tok_grouped[0], images)
-        wk = quantise(wk_grouped, weights)
-        wv_grouped = transpose_weight(wv_raw)
-        tok_grouped.append(regroup_token(1))
         wv = quantise(wv_grouped, weights)
+        wk_grouped = transpose_weight(wk_raw)
+        tok_grouped.append(regroup_token(1))
+        wk = quantise(wk_grouped, weights)
+        tok[1] = quantise(tok_grouped[1], images)
+        for i in range(CHUNKS):
+            value_chunk(0, i)
         for i in range(CHUNKS):
             sumsq_chunk(0, i)
-        tok[1] = quantise(tok_grouped[1], images)
         tok_grouped.append(regroup_token(2))
         for b in range(IMAGES):
-            for i in range(CHUNKS):
-                value_chunk(b, i)
             if b + 2 < IMAGES:
                 tok[b + 2] = quantise(tok_grouped[b + 2], images)
             if b + 3 < IMAGES:
                 tok_grouped.append(regroup_token(b + 3))
+            if b + 1 < IMAGES:
+                for i in range(CHUNKS):
+                    value_chunk(b + 1, i)
             spread_inverse_norm(b)
             for i in range(CHUNKS):
                 key_chunk(b, i)

@@ -23,23 +23,31 @@ FLOPS = 2 * 2 * IMAGES * OUT_CH * IN_CH * PIXELS
 def tile_trgramkqv_pa_kernel(tc, token, Wk, Wv, out_0, out_1):
     nc = tc.nc
     kn_out, vf_out = out_0, out_1
+    MULT = mybir.AluOpType.mult
+    ADD = mybir.AluOpType.add
 
     with tc.tile_pool(name="consts", bufs=1) as consts, tc.tile_pool(
         name="weights", bufs=2
     ) as weights, tc.tile_pool(name="images", bufs=IMAGES) as images, tc.psum_pool(
         name="to_scalar", bufs=4
     ) as to_scalar, tc.psum_pool(name="to_vector", bufs=4) as to_vector, tc.manual_schedule():
-        wv_raw = weights.tile([P, CHUNKS * IN_CH], BF16, name="w_raw", tag="w_raw")
-        nc.sync.dma_start(
-            out=wv_raw[:].rearrange("p (j k) -> p j k", j=CHUNKS),
-            in_=Wv.rearrange("(j p) k -> p j k", p=P),
-        )
         tok_raw = [images.tile([P, PACK * PIXELS], BF16, name="tok_raw", tag="tok_raw") for b in range(IMAGES)]
-        nc.sync.dma_start(out=tok_raw[0][:], in_=token[0].rearrange("(p t) h w -> p (t h w)", t=PACK))
-        wk_raw = weights.tile([P, CHUNKS * IN_CH], BF16, name="w_raw", tag="w_raw")
-        nc.sync.dma_start(out=wk_raw[:], in_=Wk.rearrange("(p j) k -> p (j k)", j=CHUNKS))
-        for b in range(1, IMAGES):
+
+        def load_token(b):
             nc.sync.dma_start(out=tok_raw[b][:], in_=token[b].rearrange("(p t) h w -> p (t h w)", t=PACK))
+
+        load_token(0)
+        wv_rows = Wv.rearrange("(j p) k -> p j k", p=P)
+        wk_rows = Wk.rearrange("(p j) k -> p j k", j=CHUNKS)
+        wv_raw = [images.tile([P, 2 * IN_CH], BF16, name="w_raw", tag="w_raw") for half in range(2)]
+        wk_raw = [images.tile([P, 2 * IN_CH], BF16, name="w_raw", tag="w_raw") for half in range(2)]
+        for raw, rows in ((wv_raw, wv_rows), (wk_raw, wk_rows)):
+            for half in range(2):
+                nc.sync.dma_start(
+                    out=raw[half][:].rearrange("p (j k) -> p j k", j=2), in_=rows[:, 2 * half : 2 * half + 2, :]
+                )
+        for b in range(1, IMAGES):
+            load_token(b)
 
         ident = consts.tile([P, P], F32)
         make_identity(nc, ident[:])
@@ -50,29 +58,41 @@ def tile_trgramkqv_pa_kernel(tc, token, Wk, Wv, out_0, out_1):
         nc.scalar.activation(out=warm[:], in_=one[:], func=ACT.Abs_reciprocal_sqrt)
 
         def transpose_weight(raw):
-            words = raw[:].bitcast(F32).rearrange("c (j p u) -> c j u p", j=CHUNKS, u=2)
             grouped = weights.tile([P, OUT_CH * PACK], BF16, align_bytes=64, name="w_grouped", tag="w_grouped")
             grouped_words = grouped[:].bitcast(F32).rearrange("p (c u) -> p c u", u=2)
             for half in range(2):
+                words = raw[half][:].bitcast(F32).rearrange("c (j p u) -> c j u p", j=2, u=2)
                 bank = to_scalar.tile([P, 2, 2 * P], F32, name="w_bank", tag="bank")
                 for jj in range(2):
                     for u in range(2):
-                        nc.tensor.transpose(
-                            bank[:, u, P * jj : P * (jj + 1)], words[:, 2 * half + jj, u, :], ident[:]
-                        )
+                        nc.tensor.transpose(bank[:, u, P * jj : P * (jj + 1)], words[:, jj, u, :], ident[:])
                 nc.scalar.copy(
                     out=grouped_words[:, 2 * P * half : 2 * P * (half + 1), :],
                     in_=bank[:].rearrange("p u c -> p c u"),
                 )
             return grouped
 
-        def regroup_token(b):
-            grouped = images.tile([P, PIXELS * PACK], BF16, align_bytes=64, name="tok_grouped", tag="tok_grouped")
+        tok_grouped = {}
+
+        def regroup_on_vector(b, pool, tag):
+            grouped = pool.tile([P, PIXELS * PACK], BF16, align_bytes=64, name=tag, tag=tag)
             nc.vector.tensor_copy(
                 out=grouped[:].rearrange("p (c i t) -> p c t i", i=4, t=PACK),
                 in_=tok_raw[b][:].rearrange("p (t c i) -> p c t i", t=PACK, i=4),
             )
-            return grouped
+            tok_grouped[b] = grouped
+
+        def regroup_on_gpsimd(b):
+            grouped = consts.tile([P, PIXELS * PACK], BF16, align_bytes=64, name="chain", tag="chain")
+            nc.gpsimd.tensor_scalar(
+                out=grouped[:].rearrange("p (c t) -> p c t", t=PACK),
+                in0=tok_raw[b][:].rearrange("p (t c) -> p c t", t=PACK),
+                scalar1=1.0,
+                scalar2=0.0,
+                op0=MULT,
+                op1=ADD,
+            )
+            tok_grouped[b] = grouped
 
         def quantise(grouped, pool):
             codes = pool.tile([P, 512], U32, align_bytes=64, name="codes", tag="codes")
@@ -92,27 +112,28 @@ def tile_trgramkqv_pa_kernel(tc, token, Wk, Wv, out_0, out_1):
             )
 
         tok = {}
+        w = {}
         v_sb = [images.tile([P, CHUNKS, OUT_CH], F32, name="v_sb", tag="v_sb") for b in range(IMAGES)]
         kn_sb = [images.tile([P, CHUNKS, PIXELS], F32, name="kn_sb", tag="kn_sb") for b in range(IMAGES)]
         squares = [images.tile([P, CHUNKS, OUT_CH], F32, name="squares", tag="squares") for b in range(IMAGES)]
         sumsq = [images.tile([P, CHUNKS], F32, name="sumsq", tag="sumsq") for b in range(IMAGES)]
         inv_row = [images.tile([P, PIXELS], F32, name="inv_row", tag="inv_row") for b in range(IMAGES)]
 
-        def value_chunk(b, i):
+        def value_chunk(b, i, on_scalar):
             pixels = slice(P * i, P * (i + 1))
-            if i >= CHUNKS // 2:
-                acc = to_vector.tile([P, OUT_CH], F32, name="v_acc", tag="bank")
-                product(acc, tok[b], pixels, wv)
-                nc.vector.tensor_copy(out=v_sb[b][:, i, :], in_=acc[:])
-            else:
+            if on_scalar:
                 acc = to_scalar.tile([P, OUT_CH], F32, name="v_acc", tag="bank")
-                product(acc, tok[b], pixels, wv)
+                product(acc, tok[b], pixels, w["v"])
                 nc.scalar.copy(out=v_sb[b][:, i, :], in_=acc[:])
+            else:
+                acc = to_vector.tile([P, OUT_CH], F32, name="v_acc", tag="bank")
+                product(acc, tok[b], pixels, w["v"])
+                nc.vector.tensor_copy(out=v_sb[b][:, i, :], in_=acc[:])
             nc.sync.dma_start(out=vf_out[b, pixels, :], in_=v_sb[b][:, i, :])
 
         def sumsq_chunk(b, i):
             acc = to_scalar.tile([P, OUT_CH], F32, name="kt_acc", tag="bank")
-            product(acc, tok[b], slice(P * i, P * (i + 1)), wk)
+            product(acc, tok[b], slice(P * i, P * (i + 1)), w["k"])
             nc.scalar.activation(
                 out=squares[b][:, i, :], in_=acc[:], func=ACT.Square, accum_out=sumsq[b][:, i : i + 1]
             )
@@ -127,42 +148,57 @@ def tile_trgramkqv_pa_kernel(tc, token, Wk, Wv, out_0, out_1):
 
         def key_chunk(b, j):
             acc = to_vector.tile([P, PIXELS], F32, name="k_acc", tag="bank")
-            product(acc, wk, slice(P * j, P * (j + 1)), tok[b])
+            product(acc, w["k"], slice(P * j, P * (j + 1)), tok[b])
             nc.vector.scalar_tensor_tensor(
                 out=kn_sb[b][:, j, :],
                 in0=inv_row[b][:],
                 scalar=1.0 / EPS,
                 in1=acc[:],
                 op0=mybir.AluOpType.min,
-                op1=mybir.AluOpType.mult,
+                op1=MULT,
             )
             if j % 2 == 1:
                 kn_rows = kn_out[b].rearrange("(p j) n -> p j n", j=CHUNKS)
                 nc.sync.dma_start(out=kn_rows[:, j - 1 : j + 1, :], in_=kn_sb[b][:, j - 1 : j + 1, :])
 
+        def quantise_token(b):
+            tok[b] = quantise(tok_grouped[b], images)
+
+        def alternate(scalar_items, vector_items):
+            for n in range(max(len(scalar_items), len(vector_items))):
+                for items in (scalar_items, vector_items):
+                    if n < len(items):
+                        fn = items[n][0]
+                        fn(*items[n][1:])
+
+        SCALAR_VALUE = 1
+        regroup_on_vector(0, consts, "first")
         wv_grouped = transpose_weight(wv_raw)
-        tok_grouped = [regroup_token(0)]
-        tok[0] = quantise(tok_grouped[0], images)
-        wv = quantise(wv_grouped, weights)
+        quantise_token(0)
+        w["v"] = quantise(wv_grouped, weights)
         wk_grouped = transpose_weight(wk_raw)
-        tok_grouped.append(regroup_token(1))
-        wk = quantise(wk_grouped, weights)
-        tok[1] = quantise(tok_grouped[1], images)
-        for i in range(CHUNKS):
-            value_chunk(0, i)
-        for i in range(CHUNKS):
-            sumsq_chunk(0, i)
-        tok_grouped.append(regroup_token(2))
+        value_chunk(0, 0, True)
+        regroup_on_vector(1, consts, "chain")
+        value_chunk(0, 1, True)
+        w["k"] = quantise(wk_grouped, weights)
+        value_chunk(0, 2, True)
+        quantise_token(1)
+        sumsq_chunk(0, 0)
         for b in range(IMAGES):
             if b + 2 < IMAGES:
-                tok[b + 2] = quantise(tok_grouped[b + 2], images)
-            if b + 3 < IMAGES:
-                tok_grouped.append(regroup_token(b + 3))
+                regroup_on_gpsimd(b + 2)
+            scalar_items = [(sumsq_chunk, b, i) for i in range(1, CHUNKS)]
             if b + 1 < IMAGES:
-                for i in range(CHUNKS):
-                    value_chunk(b + 1, i)
-            spread_inverse_norm(b)
-            for i in range(CHUNKS):
-                key_chunk(b, i)
-                if b + 1 < IMAGES:
-                    sumsq_chunk(b + 1, i)
+                scalar_items += [(sumsq_chunk, b + 1, 0), (value_chunk, b + 1, SCALAR_VALUE, True)]
+            scalar_items += [(spread_inverse_norm, b)]
+            if b == 0:
+                vector_items = [(value_chunk, 0, 3, False)]
+            else:
+                vector_items = [(key_chunk, b - 1, j) for j in range(CHUNKS)]
+            if b + 1 < IMAGES:
+                vector_items += [(value_chunk, b + 1, i, False) for i in range(CHUNKS) if i != SCALAR_VALUE]
+            if b + 2 < IMAGES:
+                vector_items += [(quantise_token, b + 2)]
+            alternate(scalar_items, vector_items)
+        for j in range(CHUNKS):
+            key_chunk(IMAGES - 1, j)

@@ -57,6 +57,14 @@ def tile_trgramkqv_pa_kernel(tc, token, Wk, Wv, out_0, out_1):
         warm = consts.tile([P, 1], F32)
         nc.scalar.activation(out=warm[:], in_=one[:], func=ACT.Abs_reciprocal_sqrt)
 
+        zeros = consts.tile([P, 512], BF16)
+        nc.vector.memset(zeros[:], 0.0)
+        unread = to_vector.tile([P, 512], F32, name="unread", tag="bank")
+
+        def busy_tensor(count):
+            for r in range(count):
+                nc.tensor.matmul(out=unread[:], lhsT=zeros[:, 0:P], rhs=zeros[:], start=True, stop=True)
+
         def transpose_weight(raw):
             grouped = weights.tile([P, OUT_CH * PACK], BF16, align_bytes=64, name="w_grouped", tag="w_grouped")
             grouped_words = grouped[:].bitcast(F32).rearrange("p (c u) -> p c u", u=2)
@@ -172,11 +180,14 @@ def tile_trgramkqv_pa_kernel(tc, token, Wk, Wv, out_0, out_1):
                         fn(*items[n][1:])
 
         SCALAR_VALUE = 1
+        busy_tensor(8)
         regroup_on_vector(0, consts, "first")
         wv_grouped = transpose_weight(wv_raw)
+        busy_tensor(2)
         quantise_token(0)
         w["v"] = quantise(wv_grouped, weights)
         wk_grouped = transpose_weight(wk_raw)
+        busy_tensor(2)
         value_chunk(0, 0, True)
         regroup_on_vector(1, consts, "chain")
         value_chunk(0, 1, True)

@@ -28,7 +28,9 @@ def tile_trgramkqv_pa_kernel(tc, token, Wk, Wv, out_0, out_1):
 
     with tc.tile_pool(name="consts", bufs=1) as consts, tc.tile_pool(
         name="weights", bufs=2
-    ) as weights, tc.tile_pool(name="images", bufs=IMAGES) as images, tc.psum_pool(
+    ) as weights, tc.tile_pool(name="images", bufs=IMAGES) as images, tc.tile_pool(
+        name="slots", bufs=2 * CHUNKS
+    ) as slots, tc.psum_pool(
         name="to_scalar", bufs=4
     ) as to_scalar, tc.psum_pool(name="to_vector", bufs=4) as to_vector, tc.manual_schedule():
         tok_raw = [images.tile([P, PACK * PIXELS], BF16, name="tok_raw", tag="tok_raw") for b in range(IMAGES)]
@@ -39,13 +41,11 @@ def tile_trgramkqv_pa_kernel(tc, token, Wk, Wv, out_0, out_1):
         load_token(0)
         wv_rows = Wv.rearrange("(j p) k -> p j k", p=P)
         wk_rows = Wk.rearrange("(p j) k -> p j k", j=CHUNKS)
-        wv_raw = [images.tile([P, 2 * IN_CH], BF16, name="w_raw", tag="w_raw") for half in range(2)]
-        wk_raw = [images.tile([P, 2 * IN_CH], BF16, name="w_raw", tag="w_raw") for half in range(2)]
+        wv_raw = [slots.tile([P, IN_CH], BF16, name="w_raw", tag="w_raw") for j in range(CHUNKS)]
+        wk_raw = [slots.tile([P, IN_CH], BF16, name="w_raw", tag="w_raw") for j in range(CHUNKS)]
         for raw, rows in ((wv_raw, wv_rows), (wk_raw, wk_rows)):
-            for half in range(2):
-                nc.sync.dma_start(
-                    out=raw[half][:].rearrange("p (j k) -> p j k", j=2), in_=rows[:, 2 * half : 2 * half + 2, :]
-                )
+            for j in range(CHUNKS):
+                nc.sync.dma_start(out=raw[j][:], in_=rows[:, j, :])
         for b in range(1, IMAGES):
             load_token(b)
 
@@ -68,15 +68,13 @@ def tile_trgramkqv_pa_kernel(tc, token, Wk, Wv, out_0, out_1):
         def transpose_weight(raw):
             grouped = weights.tile([P, OUT_CH * PACK], BF16, align_bytes=64, name="w_grouped", tag="w_grouped")
             grouped_words = grouped[:].bitcast(F32).rearrange("p (c u) -> p c u", u=2)
-            for half in range(2):
-                words = raw[half][:].bitcast(F32).rearrange("c (j p u) -> c j u p", j=2, u=2)
-                bank = to_scalar.tile([P, 2, 2 * P], F32, name="w_bank", tag="bank")
-                for jj in range(2):
-                    for u in range(2):
-                        nc.tensor.transpose(bank[:, u, P * jj : P * (jj + 1)], words[:, jj, u, :], ident[:])
+            for j in range(CHUNKS):
+                words = raw[j][:].bitcast(F32).rearrange("c (p u) -> c u p", u=2)
+                bank = to_scalar.tile([P, 2, P], F32, name="w_bank", tag="bank")
+                for u in range(2):
+                    nc.tensor.transpose(bank[:, u, :], words[:, u, :], ident[:])
                 nc.scalar.copy(
-                    out=grouped_words[:, 2 * P * half : 2 * P * (half + 1), :],
-                    in_=bank[:].rearrange("p u c -> p c u"),
+                    out=grouped_words[:, P * j : P * (j + 1), :], in_=bank[:].rearrange("p u c -> p c u")
                 )
             return grouped
 
@@ -89,6 +87,16 @@ def tile_trgramkqv_pa_kernel(tc, token, Wk, Wv, out_0, out_1):
                 in_=tok_raw[b][:].rearrange("p (t c i) -> p c t i", t=PACK, i=4),
             )
             tok_grouped[b] = grouped
+
+        def regroup_half(b, half):
+            columns = slice(PIXELS * PACK // 2 * half, PIXELS * PACK // 2 * (half + 1))
+            pixels = slice(PIXELS // 2 * half, PIXELS // 2 * (half + 1))
+            nc.vector.tensor_copy(
+                out=tok_grouped[b][:, columns].rearrange("p (c i t) -> p c t i", i=4, t=PACK),
+                in_=tok_raw[b][:].rearrange("p (t n) -> p t n", t=PACK)[:, :, pixels].rearrange(
+                    "p t (c i) -> p c t i", i=4
+                ),
+            )
 
         def regroup_on_gpsimd(b):
             grouped = consts.tile([P, PIXELS * PACK], BF16, align_bytes=64, name="chain", tag="chain")
@@ -107,6 +115,19 @@ def tile_trgramkqv_pa_kernel(tc, token, Wk, Wv, out_0, out_1):
             scales = pool.tile([P, 512], U8, align_bytes=64, name="scales", tag="scales")
             nc.vector.quantize_mx(out=codes[:].bitcast(FP8X4), scales=scales[:], in_=grouped[:])
             return codes, scales
+
+        def new_operand(pool):
+            codes = pool.tile([P, 512], U32, align_bytes=64, name="codes", tag="codes")
+            scales = pool.tile([P, 512], U8, align_bytes=64, name="scales", tag="scales")
+            return codes, scales
+
+        def quantise_half(grouped, operand, half):
+            columns = slice(256 * half, 256 * (half + 1))
+            nc.vector.quantize_mx(
+                out=operand[0][:, columns].bitcast(FP8X4),
+                scales=operand[1][:, columns],
+                in_=grouped[:, 256 * PACK * half : 256 * PACK * (half + 1)],
+            )
 
         def product(acc, stationary, columns, moving):
             nc.tensor.matmul_mx(
@@ -181,17 +202,24 @@ def tile_trgramkqv_pa_kernel(tc, token, Wk, Wv, out_0, out_1):
 
         SCALAR_VALUE = 1
         busy_tensor(8)
-        regroup_on_vector(0, consts, "first")
+        tok_grouped[0] = consts.tile([P, PIXELS * PACK], BF16, align_bytes=64, name="first", tag="first")
+        tok[0] = new_operand(images)
+        w["v"] = new_operand(weights)
+        w["k"] = new_operand(weights)
+        regroup_half(0, 0)
+        regroup_half(0, 1)
         wv_grouped = transpose_weight(wv_raw)
         busy_tensor(2)
-        quantise_token(0)
-        w["v"] = quantise(wv_grouped, weights)
+        quantise_half(tok_grouped[0], tok[0], 0)
+        quantise_half(wv_grouped, w["v"], 0)
+        quantise_half(tok_grouped[0], tok[0], 1)
+        quantise_half(wv_grouped, w["v"], 1)
         wk_grouped = transpose_weight(wk_raw)
-        busy_tensor(2)
         value_chunk(0, 0, True)
-        regroup_on_vector(1, consts, "chain")
+        quantise_half(wk_grouped, w["k"], 0)
         value_chunk(0, 1, True)
-        w["k"] = quantise(wk_grouped, weights)
+        quantise_half(wk_grouped, w["k"], 1)
+        regroup_on_vector(1, consts, "chain")
         value_chunk(0, 2, True)
         quantise_token(1)
         sumsq_chunk(0, 0)

@@ -36,7 +36,10 @@ def tile_trgramkqv_pa_kernel(tc, token, Wk, Wv, out_0, out_1):
         tok_raw = [images.tile([P, PACK * PIXELS], BF16, name="tok_raw", tag="tok_raw") for b in range(IMAGES)]
 
         def load_token(b):
-            nc.sync.dma_start(out=tok_raw[b][:], in_=token[b].rearrange("(p t) h w -> p (t h w)", t=PACK))
+            nc.sync.dma_start(
+                out=tok_raw[b][:].rearrange("p (u x) -> p u x", u=2),
+                in_=token[b].rearrange("(u p e) h w -> p u (e h w)", u=2, e=2),
+            )
 
         load_token(0)
         wv_rows = Wv.rearrange("(j p) k -> p j k", p=P)
@@ -69,7 +72,7 @@ def tile_trgramkqv_pa_kernel(tc, token, Wk, Wv, out_0, out_1):
             grouped = weights.tile([P, OUT_CH * PACK], BF16, align_bytes=64, name="w_grouped", tag="w_grouped")
             grouped_words = grouped[:].bitcast(F32).rearrange("p (c u) -> p c u", u=2)
             for j in range(CHUNKS):
-                words = raw[j][:].bitcast(F32).rearrange("c (p u) -> c u p", u=2)
+                words = raw[j][:].bitcast(F32).rearrange("c (u p) -> c u p", u=2)
                 bank = to_scalar.tile([P, 2, P], F32, name="w_bank", tag="bank")
                 for u in range(2):
                     nc.tensor.transpose(bank[:, u, :], words[:, u, :], ident[:])
@@ -148,6 +151,8 @@ def tile_trgramkqv_pa_kernel(tc, token, Wk, Wv, out_0, out_1):
         sumsq = [images.tile([P, CHUNKS], F32, name="sumsq", tag="sumsq") for b in range(IMAGES)]
         inv_row = [images.tile([P, PIXELS], F32, name="inv_row", tag="inv_row") for b in range(IMAGES)]
 
+        values_done = set()
+
         def value_chunk(b, i, on_scalar):
             pixels = slice(P * i, P * (i + 1))
             if on_scalar:
@@ -158,7 +163,13 @@ def tile_trgramkqv_pa_kernel(tc, token, Wk, Wv, out_0, out_1):
                 acc = to_vector.tile([P, OUT_CH], F32, name="v_acc", tag="bank")
                 product(acc, tok[b], pixels, w["v"])
                 nc.vector.tensor_copy(out=v_sb[b][:, i, :], in_=acc[:])
-            nc.sync.dma_start(out=vf_out[b, pixels, :], in_=v_sb[b][:, i, :])
+            values_done.add((b, i))
+            if b < 2:
+                nc.sync.dma_start(out=vf_out[b, pixels, :], in_=v_sb[b][:, i, :])
+            elif (b, i + 1 - 2 * (i % 2)) in values_done:
+                first = i - i % 2
+                vf_rows = vf_out[b].rearrange("(i p) c -> p i c", p=P)
+                nc.sync.dma_start(out=vf_rows[:, first : first + 2, :], in_=v_sb[b][:, first : first + 2, :])
 
         def sumsq_chunk(b, i):
             acc = to_scalar.tile([P, OUT_CH], F32, name="kt_acc", tag="bank")
@@ -186,8 +197,10 @@ def tile_trgramkqv_pa_kernel(tc, token, Wk, Wv, out_0, out_1):
                 op0=mybir.AluOpType.min,
                 op1=MULT,
             )
-            if j % 2 == 1:
-                kn_rows = kn_out[b].rearrange("(p j) n -> p j n", j=CHUNKS)
+            kn_rows = kn_out[b].rearrange("(p j) n -> p j n", j=CHUNKS)
+            if b == 0:
+                nc.sync.dma_start(out=kn_rows[:, j, :], in_=kn_sb[b][:, j, :])
+            elif j % 2 == 1:
                 nc.sync.dma_start(out=kn_rows[:, j - 1 : j + 1, :], in_=kn_sb[b][:, j - 1 : j + 1, :])
 
         def quantise_token(b):

@@ -209,7 +209,7 @@ def tile_trgramkqv_pa_kernel(tc, token, Wk, Wv, out_0, out_1):
         def alternate(scalar_items, vector_items):
             for n in range(max(len(scalar_items), len(vector_items))):
                 for items in (scalar_items, vector_items):
-                    if n < len(items):
+                    if n < len(items) and items[n] is not None:
                         fn = items[n][0]
                         fn(*items[n][1:])
 
@@ -232,10 +232,14 @@ def tile_trgramkqv_pa_kernel(tc, token, Wk, Wv, out_0, out_1):
         quantise_half(wk_grouped, w["k"], 0)
         value_chunk(0, 1, True)
         quantise_half(wk_grouped, w["k"], 1)
-        regroup_on_vector(1, consts, "chain")
+        tok_grouped[1] = consts.tile([P, PIXELS * PACK], BF16, align_bytes=64, name="chain", tag="chain")
+        tok[1] = new_operand(images)
+        regroup_half(1, 0)
         value_chunk(0, 2, True)
-        quantise_token(1)
+        regroup_half(1, 1)
         sumsq_chunk(0, 0)
+        quantise_half(tok_grouped[1], tok[1], 0)
+        quantise_half(tok_grouped[1], tok[1], 1)
         for b in range(IMAGES):
             if b + 2 < IMAGES:
                 regroup_on_gpsimd(b + 2)
@@ -244,7 +248,7 @@ def tile_trgramkqv_pa_kernel(tc, token, Wk, Wv, out_0, out_1):
                 scalar_items += [(sumsq_chunk, b + 1, 0), (value_chunk, b + 1, SCALAR_VALUE, True)]
             scalar_items += [(spread_inverse_norm, b)]
             if b == 0:
-                vector_items = [(value_chunk, 0, 3, False)]
+                vector_items = [(value_chunk, 0, 3, False), None]
             else:
                 vector_items = [(key_chunk, b - 1, j) for j in range(CHUNKS)]
             if b + 1 < IMAGES:

@@ -29,7 +29,7 @@ def tile_trgramkqv_pa_kernel(tc, token, Wk, Wv, out_0, out_1):
     with tc.tile_pool(name="consts", bufs=1) as consts, tc.tile_pool(
         name="weights", bufs=2
     ) as weights, tc.tile_pool(name="images", bufs=IMAGES) as images, tc.tile_pool(
-        name="slots", bufs=2 * CHUNKS
+        name="slots", bufs=4
     ) as slots, tc.psum_pool(
         name="to_scalar", bufs=4
     ) as to_scalar, tc.psum_pool(name="to_vector", bufs=4) as to_vector, tc.manual_schedule():
@@ -42,13 +42,13 @@ def tile_trgramkqv_pa_kernel(tc, token, Wk, Wv, out_0, out_1):
             )
 
         load_token(0)
-        wv_rows = Wv.rearrange("(j p) k -> p j k", p=P)
-        wk_rows = Wk.rearrange("(p j) k -> p j k", j=CHUNKS)
-        wv_raw = [slots.tile([P, IN_CH], BF16, name="w_raw", tag="w_raw") for j in range(CHUNKS)]
-        wk_raw = [slots.tile([P, IN_CH], BF16, name="w_raw", tag="w_raw") for j in range(CHUNKS)]
+        wv_rows = Wv.rearrange("(h p e) k -> h p e k", h=2, e=2)
+        wk_rows = Wk.rearrange("(p h e) k -> h p e k", h=2, e=2)
+        wv_raw = [slots.tile([P, 2, IN_CH], BF16, name="w_raw", tag="w_raw") for h in range(2)]
+        wk_raw = [slots.tile([P, 2, IN_CH], BF16, name="w_raw", tag="w_raw") for h in range(2)]
         for raw, rows in ((wv_raw, wv_rows), (wk_raw, wk_rows)):
-            for j in range(CHUNKS):
-                nc.sync.dma_start(out=raw[j][:], in_=rows[:, j, :])
+            for h in range(2):
+                nc.sync.dma_start(out=raw[h][:], in_=rows[h])
         for b in range(1, IMAGES):
             load_token(b)
 
@@ -64,21 +64,33 @@ def tile_trgramkqv_pa_kernel(tc, token, Wk, Wv, out_0, out_1):
         nc.vector.memset(zeros[:], 0.0)
         unread = to_vector.tile([P, 512], F32, name="unread", tag="bank")
 
-        def busy_tensor(count):
+        def busy_tensor(count, columns):
             for r in range(count):
-                nc.tensor.matmul(out=unread[:], lhsT=zeros[:, 0:P], rhs=zeros[:], start=True, stop=True)
-
-        def transpose_weight(raw):
-            grouped = weights.tile([P, OUT_CH * PACK], BF16, align_bytes=64, name="w_grouped", tag="w_grouped")
-            grouped_words = grouped[:].bitcast(F32).rearrange("p (c u) -> p c u", u=2)
-            for j in range(CHUNKS):
-                words = raw[j][:].bitcast(F32).rearrange("c (u p) -> c u p", u=2)
-                bank = to_scalar.tile([P, 2, P], F32, name="w_bank", tag="bank")
-                for u in range(2):
-                    nc.tensor.transpose(bank[:, u, :], words[:, u, :], ident[:])
-                nc.scalar.copy(
-                    out=grouped_words[:, P * j : P * (j + 1), :], in_=bank[:].rearrange("p u c -> p c u")
+                nc.tensor.matmul(
+                    out=unread[:, 0:columns], lhsT=zeros[:, 0:P], rhs=zeros[:, 0:columns], start=True, stop=True
                 )
+
+        def transpose_weight(raw, pairs_side_by_side):
+            grouped = weights.tile([P, OUT_CH * PACK], BF16, align_bytes=64, name="w_grouped", tag="w_grouped")
+            grouped_words = grouped[:].bitcast(F32)
+            for h in range(2):
+                bank = to_scalar.tile([P, 4, P], F32, name="w_bank", tag="bank")
+                for e in range(2):
+                    words = raw[h][:, e, :].bitcast(F32)
+                    for u in range(2):
+                        nc.tensor.transpose(bank[:, 2 * e + u, :], words[:, P * u : P * (u + 1)], ident[:])
+                half = grouped_words[:, 512 * h : 512 * (h + 1)]
+                if pairs_side_by_side:
+                    nc.scalar.copy(
+                        out=half.rearrange("p (q e u) -> p q e u", e=2, u=2),
+                        in_=bank[:].rearrange("p (e u) q -> p q e u", e=2),
+                    )
+                else:
+                    nc.scalar.copy(
+                        out=half.rearrange("p (e q u) -> p e q u", e=2, u=2),
+                        in_=bank[:].rearrange("p (e u) q -> p e q u", e=2),
+                    )
+                busy_tensor(1, 256)
             return grouped
 
         tok_grouped = {}
@@ -214,20 +226,19 @@ def tile_trgramkqv_pa_kernel(tc, token, Wk, Wv, out_0, out_1):
                         fn(*items[n][1:])
 
         SCALAR_VALUE = 1
-        busy_tensor(8)
+        busy_tensor(8, 512)
         tok_grouped[0] = consts.tile([P, PIXELS * PACK], BF16, align_bytes=64, name="first", tag="first")
         tok[0] = new_operand(images)
         w["v"] = new_operand(weights)
         w["k"] = new_operand(weights)
         regroup_half(0, 0)
         regroup_half(0, 1)
-        wv_grouped = transpose_weight(wv_raw)
-        busy_tensor(2)
+        wv_grouped = transpose_weight(wv_raw, True)
         quantise_half(tok_grouped[0], tok[0], 0)
         quantise_half(wv_grouped, w["v"], 0)
         quantise_half(tok_grouped[0], tok[0], 1)
         quantise_half(wv_grouped, w["v"], 1)
-        wk_grouped = transpose_weight(wk_raw)
+        wk_grouped = transpose_weight(wk_raw, False)
         value_chunk(0, 0, True)
         quantise_half(wk_grouped, w["k"], 0)
         value_chunk(0, 1, True)

@@ -90,7 +90,7 @@ def tile_trgramkqv_pa_kernel(tc, token, Wk, Wv, out_0, out_1):
                         out=half.rearrange("p (e q u) -> p e q u", e=2, u=2),
                         in_=bank[:].rearrange("p (e u) q -> p e q u", e=2),
                     )
-                busy_tensor(1, 256)
+                busy_tensor(1, 512)
             return grouped
 
         tok_grouped = {}

@@ -70,7 +70,7 @@ def tile_trgramkqv_pa_kernel(tc, token, Wk, Wv, out_0, out_1):
                     out=unread[:, 0:columns], lhsT=zeros[:, 0:P], rhs=zeros[:, 0:columns], start=True, stop=True
                 )
 
-        def transpose_weight(raw, pairs_side_by_side):
+        def transpose_weight(raw, pairs_side_by_side, busy_between):
             grouped = weights.tile([P, OUT_CH * PACK], BF16, align_bytes=64, name="w_grouped", tag="w_grouped")
             grouped_words = grouped[:].bitcast(F32)
             for h in range(2):
@@ -90,7 +90,8 @@ def tile_trgramkqv_pa_kernel(tc, token, Wk, Wv, out_0, out_1):
                         out=half.rearrange("p (e q u) -> p e q u", e=2, u=2),
                         in_=bank[:].rearrange("p (e u) q -> p e q u", e=2),
                     )
-                busy_tensor(1, 512)
+                if busy_between:
+                    busy_tensor(1, 512)
             return grouped
 
         tok_grouped = {}
@@ -218,14 +219,6 @@ def tile_trgramkqv_pa_kernel(tc, token, Wk, Wv, out_0, out_1):
         def quantise_token(b):
             tok[b] = quantise(tok_grouped[b], images)
 
-        def alternate(scalar_items, vector_items):
-            for n in range(max(len(scalar_items), len(vector_items))):
-                for items in (scalar_items, vector_items):
-                    if n < len(items) and items[n] is not None:
-                        fn = items[n][0]
-                        fn(*items[n][1:])
-
-        SCALAR_VALUE = 1
         busy_tensor(8, 512)
         tok_grouped[0] = consts.tile([P, PIXELS * PACK], BF16, align_bytes=64, name="first", tag="first")
         tok[0] = new_operand(images)
@@ -233,16 +226,16 @@ def tile_trgramkqv_pa_kernel(tc, token, Wk, Wv, out_0, out_1):
         w["k"] = new_operand(weights)
         regroup_half(0, 0)
         regroup_half(0, 1)
-        wv_grouped = transpose_weight(wv_raw, True)
+        wv_grouped = transpose_weight(wv_raw, True, True)
         quantise_half(tok_grouped[0], tok[0], 0)
-        quantise_half(wv_grouped, w["v"], 0)
         quantise_half(tok_grouped[0], tok[0], 1)
+        quantise_half(wv_grouped, w["v"], 0)
         quantise_half(wv_grouped, w["v"], 1)
-        wk_grouped = transpose_weight(wk_raw, False)
-        value_chunk(0, 0, True)
+        wk_grouped = transpose_weight(wk_raw, False, False)
         quantise_half(wk_grouped, w["k"], 0)
-        value_chunk(0, 1, True)
+        value_chunk(0, 0, True)
         quantise_half(wk_grouped, w["k"], 1)
+        value_chunk(0, 1, True)
         tok_grouped[1] = consts.tile([P, PIXELS * PACK], BF16, align_bytes=64, name="chain", tag="chain")
         tok[1] = new_operand(images)
         regroup_half(1, 0)
@@ -251,21 +244,43 @@ def tile_trgramkqv_pa_kernel(tc, token, Wk, Wv, out_0, out_1):
         sumsq_chunk(0, 0)
         quantise_half(tok_grouped[1], tok[1], 0)
         quantise_half(tok_grouped[1], tok[1], 1)
-        for b in range(IMAGES):
-            if b + 2 < IMAGES:
-                regroup_on_gpsimd(b + 2)
-            scalar_items = [(sumsq_chunk, b, i) for i in range(1, CHUNKS)]
-            if b + 1 < IMAGES:
-                scalar_items += [(sumsq_chunk, b + 1, 0), (value_chunk, b + 1, SCALAR_VALUE, True)]
-            scalar_items += [(spread_inverse_norm, b)]
-            if b == 0:
-                vector_items = [(value_chunk, 0, 3, False), None]
-            else:
-                vector_items = [(key_chunk, b - 1, j) for j in range(CHUNKS)]
-            if b + 1 < IMAGES:
-                vector_items += [(value_chunk, b + 1, i, False) for i in range(CHUNKS) if i != SCALAR_VALUE]
-            if b + 2 < IMAGES:
-                vector_items += [(quantise_token, b + 2)]
-            alternate(scalar_items, vector_items)
+        regroup_on_gpsimd(2)
+        sumsq_chunk(0, 1)
+        value_chunk(0, 3, False)
+        sumsq_chunk(0, 2)
+        sumsq_chunk(0, 3)
+        value_chunk(1, 0, False)
+        sumsq_chunk(1, 0)
+        for i in range(1, CHUNKS):
+            value_chunk(1, i, False)
+        spread_inverse_norm(0)
+        quantise_token(2)
+        regroup_on_gpsimd(3)
+        for j in range(CHUNKS - 1):
+            sumsq_chunk(1, j + 1)
+            key_chunk(0, j)
+        sumsq_chunk(2, 0)
+        key_chunk(0, 3)
+        value_chunk(2, 1, True)
+        value_chunk(2, 0, False)
+        spread_inverse_norm(1)
+        value_chunk(2, 2, False)
+        value_chunk(2, 3, True)
+        quantise_token(3)
+        for j in range(CHUNKS - 1):
+            sumsq_chunk(2, j + 1)
+            key_chunk(1, j)
+        sumsq_chunk(3, 0)
+        key_chunk(1, 3)
+        value_chunk(3, 1, True)
+        value_chunk(3, 0, False)
+        spread_inverse_norm(2)
+        value_chunk(3, 2, False)
+        for j in range(CHUNKS - 1):
+            sumsq_chunk(3, j + 1)
+            key_chunk(2, j)
+        value_chunk(3, 3, True)
+        key_chunk(2, 3)
+        spread_inverse_norm(3)
         for j in range(CHUNKS):
             key_chunk(IMAGES - 1, j)

@@ -52,16 +52,16 @@ def tile_trgramkqv_pa_kernel(tc, token, Wk, Wv, out_0, out_1):
         for b in range(1, IMAGES):
             load_token(b)
 
-        ident = consts.tile([P, P], F32)
-        make_identity(nc, ident[:])
-
+        zero_words = consts.tile([P, 256], F32)
+        nc.vector.memset(zero_words[:], 0.0)
+        zeros = zero_words[:].bitcast(BF16)
         one = consts.tile([P, 1], F32)
         nc.vector.memset(one[:], 1.0)
         warm = consts.tile([P, 1], F32)
         nc.scalar.activation(out=warm[:], in_=one[:], func=ACT.Abs_reciprocal_sqrt)
+        ident = consts.tile([P, P], F32)
+        make_identity(nc, ident[:])
 
-        zeros = consts.tile([P, 512], BF16)
-        nc.vector.memset(zeros[:], 0.0)
         unread = to_vector.tile([P, 512], F32, name="unread", tag="bank")
 
         def busy_tensor(count, columns):
@@ -70,7 +70,7 @@ def tile_trgramkqv_pa_kernel(tc, token, Wk, Wv, out_0, out_1):
                     out=unread[:, 0:columns], lhsT=zeros[:, 0:P], rhs=zeros[:, 0:columns], start=True, stop=True
                 )
 
-        def transpose_weight(raw, pairs_side_by_side, busy_between):
+        def transpose_weight(raw, pairs_side_by_side, busy_columns):
             grouped = weights.tile([P, OUT_CH * PACK], BF16, align_bytes=64, name="w_grouped", tag="w_grouped")
             grouped_words = grouped[:].bitcast(F32)
             for h in range(2):
@@ -90,8 +90,8 @@ def tile_trgramkqv_pa_kernel(tc, token, Wk, Wv, out_0, out_1):
                         out=half.rearrange("p (e q u) -> p e q u", e=2, u=2),
                         in_=bank[:].rearrange("p (e u) q -> p e q u", e=2),
                     )
-                if busy_between:
-                    busy_tensor(1, 512)
+                for columns in busy_columns[h]:
+                    busy_tensor(1, columns)
             return grouped
 
         tok_grouped = {}
@@ -226,12 +226,12 @@ def tile_trgramkqv_pa_kernel(tc, token, Wk, Wv, out_0, out_1):
         w["k"] = new_operand(weights)
         regroup_half(0, 0)
         regroup_half(0, 1)
-        wv_grouped = transpose_weight(wv_raw, True, True)
+        wv_grouped = transpose_weight(wv_raw, True, ((256,), (512, 512)))
         quantise_half(tok_grouped[0], tok[0], 0)
         quantise_half(tok_grouped[0], tok[0], 1)
         quantise_half(wv_grouped, w["v"], 0)
         quantise_half(wv_grouped, w["v"], 1)
-        wk_grouped = transpose_weight(wk_raw, False, False)
+        wk_grouped = transpose_weight(wk_raw, False, ((), ()))
         quantise_half(wk_grouped, w["k"], 0)
         value_chunk(0, 0, True)
         quantise_half(wk_grouped, w["k"], 1)

import concourse.mybir as mybir
from concourse.masks import make_identity

BF16 = mybir.dt.bfloat16
F32 = mybir.dt.float32
U32 = mybir.dt.uint32
U8 = mybir.dt.uint8
FP8X4 = mybir.dt.float8_e4m3fn_x4
ACT = mybir.ActivationFunctionType

P = 128
PACK = 4
IMAGES = 4
IN_CH = P * PACK
OUT_CH = 512
PIXELS = 512
CHUNKS = 4
EPS = 1e-6

FLOPS = 2 * 2 * IMAGES * OUT_CH * IN_CH * PIXELS


def tile_trgramkqv_pa_kernel(tc, token, Wk, Wv, out_0, out_1):
    nc = tc.nc
    kn_out, vf_out = out_0, out_1
    MULT = mybir.AluOpType.mult
    ADD = mybir.AluOpType.add

    with tc.tile_pool(name="consts", bufs=1) as consts, tc.tile_pool(
        name="weights", bufs=2
    ) as weights, tc.tile_pool(name="images", bufs=IMAGES) as images, tc.tile_pool(
        name="slots", bufs=4
    ) as slots, tc.psum_pool(
        name="to_scalar", bufs=4
    ) as to_scalar, tc.psum_pool(name="to_vector", bufs=4) as to_vector, tc.manual_schedule():
        tok_raw = [images.tile([P, PACK * PIXELS], BF16, name="tok_raw", tag="tok_raw") for b in range(IMAGES)]

        def load_token(b):
            nc.sync.dma_start(
                out=tok_raw[b][:].rearrange("p (u x) -> p u x", u=2),
                in_=token[b].rearrange("(u p e) h w -> p u (e h w)", u=2, e=2),
            )

        load_token(0)
        wv_rows = Wv.rearrange("(h p e) k -> h p e k", h=2, e=2)
        wk_rows = Wk.rearrange("(p h e) k -> h p e k", h=2, e=2)
        wv_raw = [slots.tile([P, 2, IN_CH], BF16, name="w_raw", tag="w_raw") for h in range(2)]
        wk_raw = [slots.tile([P, 2, IN_CH], BF16, name="w_raw", tag="w_raw") for h in range(2)]
        for raw, rows in ((wv_raw, wv_rows), (wk_raw, wk_rows)):
            for h in range(2):
                nc.sync.dma_start(out=raw[h][:], in_=rows[h])
        for b in range(1, IMAGES):
            load_token(b)

        zero_words = consts.tile([P, 256], F32)
        nc.vector.memset(zero_words[:], 0.0)
        zeros = zero_words[:].bitcast(BF16)
        one = consts.tile([P, 1], F32)
        nc.vector.memset(one[:], 1.0)
        warm = consts.tile([P, 1], F32)
        nc.scalar.activation(out=warm[:], in_=one[:], func=ACT.Abs_reciprocal_sqrt)
        ident = consts.tile([P, P], F32)
        make_identity(nc, ident[:])

        unread = to_vector.tile([P, 512], F32, name="unread", tag="bank")

        def busy_tensor(count, columns):
            for r in range(count):
                nc.tensor.matmul(
                    out=unread[:, 0:columns], lhsT=zeros[:, 0:P], rhs=zeros[:, 0:columns], start=True, stop=True
                )

        def transpose_weight(raw, pairs_side_by_side, busy_columns):
            grouped = weights.tile([P, OUT_CH * PACK], BF16, align_bytes=64, name="w_grouped", tag="w_grouped")
            grouped_words = grouped[:].bitcast(F32)
            for h in range(2):
                bank = to_scalar.tile([P, 4, P], F32, name="w_bank", tag="bank")
                for e in range(2):
                    words = raw[h][:, e, :].bitcast(F32)
                    for u in range(2):
                        nc.tensor.transpose(bank[:, 2 * e + u, :], words[:, P * u : P * (u + 1)], ident[:])
                half = grouped_words[:, 512 * h : 512 * (h + 1)]
                if pairs_side_by_side:
                    nc.scalar.copy(
                        out=half.rearrange("p (q e u) -> p q e u", e=2, u=2),
                        in_=bank[:].rearrange("p (e u) q -> p q e u", e=2),
                    )
                else:
                    nc.scalar.copy(
                        out=half.rearrange("p (e q u) -> p e q u", e=2, u=2),
                        in_=bank[:].rearrange("p (e u) q -> p e q u", e=2),
                    )
                for columns in busy_columns[h]:
                    busy_tensor(1, columns)
            return grouped

        tok_grouped = {}

        def regroup_on_vector(b, pool, tag):
            grouped = pool.tile([P, PIXELS * PACK], BF16, align_bytes=64, name=tag, tag=tag)
            nc.vector.tensor_copy(
                out=grouped[:].rearrange("p (c i t) -> p c t i", i=4, t=PACK),
                in_=tok_raw[b][:].rearrange("p (t c i) -> p c t i", t=PACK, i=4),
            )
            tok_grouped[b] = grouped

        def regroup_half(b, half):
            columns = slice(PIXELS * PACK // 2 * half, PIXELS * PACK // 2 * (half + 1))
            pixels = slice(PIXELS // 2 * half, PIXELS // 2 * (half + 1))
            nc.vector.tensor_copy(
                out=tok_grouped[b][:, columns].rearrange("p (c i t) -> p c t i", i=4, t=PACK),
                in_=tok_raw[b][:].rearrange("p (t n) -> p t n", t=PACK)[:, :, pixels].rearrange(
                    "p t (c i) -> p c t i", i=4
                ),
            )

        def regroup_on_gpsimd(b):
            grouped = consts.tile([P, PIXELS * PACK], BF16, align_bytes=64, name="chain", tag="chain")
            nc.gpsimd.tensor_scalar(
                out=grouped[:].rearrange("p (c t) -> p c t", t=PACK),
                in0=tok_raw[b][:].rearrange("p (t c) -> p c t", t=PACK),
                scalar1=1.0,
                scalar2=0.0,
                op0=MULT,
                op1=ADD,
            )
            tok_grouped[b] = grouped

        def quantise(grouped, pool):
            codes = pool.tile([P, 512], U32, align_bytes=64, name="codes", tag="codes")
            scales = pool.tile([P, 512], U8, align_bytes=64, name="scales", tag="scales")
            nc.vector.quantize_mx(out=codes[:].bitcast(FP8X4), scales=scales[:], in_=grouped[:])
            return codes, scales

        def new_operand(pool):
            codes = pool.tile([P, 512], U32, align_bytes=64, name="codes", tag="codes")
            scales = pool.tile([P, 512], U8, align_bytes=64, name="scales", tag="scales")
            return codes, scales

        def quantise_half(grouped, operand, half):
            columns = slice(256 * half, 256 * (half + 1))
            nc.vector.quantize_mx(
                out=operand[0][:, columns].bitcast(FP8X4),
                scales=operand[1][:, columns],
                in_=grouped[:, 256 * PACK * half : 256 * PACK * (half + 1)],
            )

        def product(acc, stationary, columns, moving):
            nc.tensor.matmul_mx(
                out=acc[:],
                lhsT=stationary[0][:, columns].bitcast(FP8X4),
                lhsT_scale=stationary[1][:, columns],
                rhs=moving[0][:].bitcast(FP8X4),
                rhs_scale=moving[1][:],
                start=True,
                stop=True,
            )

        tok = {}
        w = {}
        v_sb = [images.tile([P, CHUNKS, OUT_CH], F32, name="v_sb", tag="v_sb") for b in range(IMAGES)]
        kn_sb = [images.tile([P, CHUNKS, PIXELS], F32, name="kn_sb", tag="kn_sb") for b in range(IMAGES)]
        squares = [images.tile([P, CHUNKS, OUT_CH], F32, name="squares", tag="squares") for b in range(IMAGES)]
        sumsq = [images.tile([P, CHUNKS], F32, name="sumsq", tag="sumsq") for b in range(IMAGES)]
        inv_row = [images.tile([P, PIXELS], F32, name="inv_row", tag="inv_row") for b in range(IMAGES)]

        values_done = set()

        def value_chunk(b, i, on_scalar):
            pixels = slice(P * i, P * (i + 1))
            if on_scalar:
                acc = to_scalar.tile([P, OUT_CH], F32, name="v_acc", tag="bank")
                product(acc, tok[b], pixels, w["v"])
                nc.scalar.copy(out=v_sb[b][:, i, :], in_=acc[:])
            else:
                acc = to_vector.tile([P, OUT_CH], F32, name="v_acc", tag="bank")
                product(acc, tok[b], pixels, w["v"])
                nc.vector.tensor_copy(out=v_sb[b][:, i, :], in_=acc[:])
            values_done.add((b, i))
            if b < 2:
                nc.sync.dma_start(out=vf_out[b, pixels, :], in_=v_sb[b][:, i, :])
            elif (b, i + 1 - 2 * (i % 2)) in values_done:
                first = i - i % 2
                vf_rows = vf_out[b].rearrange("(i p) c -> p i c", p=P)
                nc.sync.dma_start(out=vf_rows[:, first : first + 2, :], in_=v_sb[b][:, first : first + 2, :])

        def sumsq_chunk(b, i):
            acc = to_scalar.tile([P, OUT_CH], F32, name="kt_acc", tag="bank")
            product(acc, tok[b], slice(P * i, P * (i + 1)), w["k"])
            nc.scalar.activation(
                out=squares[b][:, i, :], in_=acc[:], func=ACT.Square, accum_out=sumsq[b][:, i : i + 1]
            )

        def spread_inverse_norm(b):
            spread = to_scalar.tile([P, PIXELS], F32, name="spread", tag="bank")
            for i in range(CHUNKS):
                nc.tensor.transpose(
                    spread[:, P * i : P * (i + 1)], sumsq[b][:, i : i + 1].to_broadcast([P, P]), ident[:]
                )
            nc.scalar.activation(out=inv_row[b][:], in_=spread[:], func=ACT.Abs_reciprocal_sqrt)

        def key_chunk(b, j):
            acc = to_vector.tile([P, PIXELS], F32, name="k_acc", tag="bank")
            product(acc, w["k"], slice(P * j, P * (j + 1)), tok[b])
            nc.vector.scalar_tensor_tensor(
                out=kn_sb[b][:, j, :],
                in0=inv_row[b][:],
                scalar=1.0 / EPS,
                in1=acc[:],
                op0=mybir.AluOpType.min,
                op1=MULT,
            )
            kn_rows = kn_out[b].rearrange("(p j) n -> p j n", j=CHUNKS)
            if b == 0:
                nc.sync.dma_start(out=kn_rows[:, j, :], in_=kn_sb[b][:, j, :])
            elif j % 2 == 1:
                nc.sync.dma_start(out=kn_rows[:, j - 1 : j + 1, :], in_=kn_sb[b][:, j - 1 : j + 1, :])

        def quantise_token(b):
            tok[b] = quantise(tok_grouped[b], images)

        busy_tensor(8, 512)
        tok_grouped[0] = consts.tile([P, PIXELS * PACK], BF16, align_bytes=64, name="first", tag="first")
        tok[0] = new_operand(images)
        w["v"] = new_operand(weights)
        w["k"] = new_operand(weights)
        regroup_half(0, 0)
        regroup_half(0, 1)
        wv_grouped = transpose_weight(wv_raw, True, ((256,), (512, 512)))
        quantise_half(tok_grouped[0], tok[0], 0)
        quantise_half(tok_grouped[0], tok[0], 1)
        quantise_half(wv_grouped, w["v"], 0)
        quantise_half(wv_grouped, w["v"], 1)
        wk_grouped = transpose_weight(wk_raw, False, ((), ()))
        quantise_half(wk_grouped, w["k"], 0)
        value_chunk(0, 0, True)
        quantise_half(wk_grouped, w["k"], 1)
        value_chunk(0, 1, True)
        tok_grouped[1] = consts.tile([P, PIXELS * PACK], BF16, align_bytes=64, name="chain", tag="chain")
        tok[1] = new_operand(images)
        regroup_half(1, 0)
        value_chunk(0, 2, True)
        regroup_half(1, 1)
        sumsq_chunk(0, 0)
        quantise_half(tok_grouped[1], tok[1], 0)
        quantise_half(tok_grouped[1], tok[1], 1)
        regroup_on_gpsimd(2)
        sumsq_chunk(0, 1)
        value_chunk(0, 3, False)
        sumsq_chunk(0, 2)
        sumsq_chunk(0, 3)
        value_chunk(1, 0, False)
        sumsq_chunk(1, 0)
        for i in range(1, CHUNKS):
            value_chunk(1, i, False)
        spread_inverse_norm(0)
        quantise_token(2)
        regroup_on_gpsimd(3)
        for j in range(CHUNKS - 1):
            sumsq_chunk(1, j + 1)
            key_chunk(0, j)
        sumsq_chunk(2, 0)
        key_chunk(0, 3)
        value_chunk(2, 1, True)
        value_chunk(2, 0, False)
        spread_inverse_norm(1)
        value_chunk(2, 2, False)
        value_chunk(2, 3, True)
        quantise_token(3)
        for j in range(CHUNKS - 1):
            sumsq_chunk(2, j + 1)
            key_chunk(1, j)
        sumsq_chunk(3, 0)
        key_chunk(1, 3)
        value_chunk(3, 1, True)
        value_chunk(3, 0, False)
        spread_inverse_norm(2)
        value_chunk(3, 2, False)
        for j in range(CHUNKS - 1):
            sumsq_chunk(3, j + 1)
            key_chunk(2, j)
        value_chunk(3, 3, True)
        key_chunk(2, 3)
        spread_inverse_norm(3)
        for j in range(CHUNKS):
            key_chunk(IMAGES - 1, j)
